import numpy as np
import ml_dtypes

BF16 = ml_dtypes.bfloat16


def bf(x):
    return np.asarray(x, np.float32).astype(BF16)


def f32(x):
    return np.asarray(x, np.float32)


def f64(x):
    return np.asarray(x).astype(np.float64)


def striped(idx):
    return np.tile(idx.reshape(-1, 16).T, (8, 1))


P, S, N = 256, 256, 256
EPS = 1e-05


def setup_inputs():
    return {"x": bf(0.5 + 1.5 * np.random.standard_normal((P, S))), "weight": bf(1.0 + 0.1 * np.random.standard_normal((1, N))), "bias": f32(0.1 * np.random.standard_normal((1, N))), "offs": striped(np.random.permutation(S)[:N])}


def reference(x, weight, bias, offs):
    idx = offs[:16].T.reshape(-1)
    xx = f64(x)
    w = f64(weight)
    mean = xx.sum() / xx.size
    var = ((xx - mean) ** 2).sum() / (xx.size - 1)
    rstd = 1.0 / np.sqrt(var + EPS)
    return (xx[:, idx] * w - mean * w) * rstd + f64(bias)

@@ -1,0 +1,72 @@
+import concourse.mybir as mybir
+
+P = 128
+ROWS, S, N = 256, 256, 256
+BLOCKS = ROWS // P
+EPS = 1e-5
+
+BF16, F32, U16 = mybir.dt.bfloat16, mybir.dt.float32, mybir.dt.uint16
+MULT, ADD = mybir.AluOpType.mult, mybir.AluOpType.add
+FUNC = mybir.ActivationFunctionType
+
+
+def tile_adaptivegroupnorm_kernel(tc, x, weight, bias, offs, out):
+    nc = tc.nc
+    with (
+        tc.tile_pool(name="held", bufs=1) as held,
+        tc.psum_pool(name="psum", bufs=1) as psum,
+    ):
+        x_bf = held.tile([P, BLOCKS * S], BF16, name="x_bf")
+        nc.sync.dma_start(x_bf[:, 0:S], x[0:P, :])
+        nc.scalar.dma_start(x_bf[:, S : 2 * S], x[P : 2 * P, :])
+        offsets = held.tile([P, N // 16], U16, name="offsets")
+        nc.sync.dma_start(offsets[:], offs)
+        weight_bf = held.tile([P, N], BF16, name="weight_bf")
+        nc.scalar.dma_start(weight_bf[:], weight.to_broadcast([P, N]))
+        bias_all = held.tile([P, N], F32, name="bias_all")
+        nc.gpsimd.dma_start(bias_all[:], bias.to_broadcast([P, N]))
+
+        minus_mean_of = held.tile([P, P], BF16, name="minus_mean_of")
+        nc.gpsimd.memset(minus_mean_of[:], -1.0 / (ROWS * S))
+        variance_of = held.tile([P, P], F32, name="variance_of")
+        nc.gpsimd.memset(variance_of[:], 1.0 / (ROWS * S - 1))
+        eps = held.tile([P, 1], F32, name="eps")
+        nc.gpsimd.memset(eps[:], EPS)
+
+        warm = held.tile([P, 1], F32, name="warm")
+        nc.scalar.activation(warm[:], eps[:], FUNC.Abs_reciprocal_sqrt)
+
+        weight_f = held.tile([P, N], F32, name="weight_f")
+        nc.gpsimd.tensor_copy(weight_f[:], weight_bf[:])
+
+        column_sums = psum.tile([P, S], F32, name="column_sums")
+        for b in range(BLOCKS):
+            nc.tensor.matmul(
+                column_sums[:], minus_mean_of[:], x_bf[:, b * S : (b + 1) * S], start=(b == 0), stop=(b == BLOCKS - 1)
+            )
+        unused_copy = held.tile([P, S], F32, name="unused_copy")
+        minus_mean = held.tile([P, 1], F32, name="minus_mean")
+        nc.scalar.activation(unused_copy[:], column_sums[:], FUNC.Copy, accum_out=minus_mean[:])
+
+        unused_squares = held.tile([P, BLOCKS * S], BF16, name="unused_squares")
+        row_squares = held.tile([P, 1], F32, name="row_squares")
+        nc.scalar.activation(unused_squares[:], x_bf[:], FUNC.Square, bias=minus_mean[:], accum_out=row_squares[:])
+        variance = psum.tile([P, 1], F32, name="variance")
+        nc.tensor.matmul(variance[:], variance_of[:], row_squares[:], start=True, stop=True)
+        rstd = held.tile([P, 1], F32, name="rstd")
+        nc.scalar.activation(rstd[:], variance[:], FUNC.Abs_reciprocal_sqrt, bias=eps[:])
+
+        blocks = range(BLOCKS)
+        x_f = [held.tile([P, S], F32, name=f"x_f{b}") for b in blocks]
+        product = [held.tile([P, N], F32, name=f"product{b}") for b in blocks]
+        centred = [held.tile([P, N], F32, name=f"centred{b}") for b in blocks]
+        result = [held.tile([P, N], F32, name=f"result{b}") for b in blocks]
+        for b in blocks:
+            nc.vector.tensor_copy(x_f[b][:], x_bf[:, b * S : (b + 1) * S])
+            nc.vector.tensor_tensor(product[b][:], x_f[b][:].indirect(offsets[:]), weight_f[:], MULT)
+        for b in blocks:
+            nc.vector.scalar_tensor_tensor(centred[b][:], weight_f[:], minus_mean[:], product[b][:], MULT, ADD)
+        store_queues = [nc.sync, nc.scalar]
+        for b in blocks:
+            nc.vector.scalar_tensor_tensor(result[b][:], centred[b][:], rstd[:], bias_all[:], MULT, ADD)
+            store_queues[b].dma_start(out[b * P : (b + 1) * P, :], result[b][:])

@@ -17,27 +17,26 @@ def tile_adaptivegroupnorm_kernel(tc, x, weight, bias, offs, out):
         tc.psum_pool(name="psum", bufs=1) as psum,
     ):
         x_bf = held.tile([P, BLOCKS * S], BF16, name="x_bf")
-        nc.sync.dma_start(x_bf[:, 0:S], x[0:P, :])
-        nc.scalar.dma_start(x_bf[:, S : 2 * S], x[P : 2 * P, :])
+        nc.sync.dma_start(x_bf[:].rearrange("p (b s) -> p b s", b=BLOCKS), x.rearrange("(b p) s -> p b s", p=P))
         offsets = held.tile([P, N // 16], U16, name="offsets")
         nc.sync.dma_start(offsets[:], offs)
         weight_bf = held.tile([P, N], BF16, name="weight_bf")
         nc.scalar.dma_start(weight_bf[:], weight.to_broadcast([P, N]))
         bias_all = held.tile([P, N], F32, name="bias_all")
-        nc.gpsimd.dma_start(bias_all[:], bias.to_broadcast([P, N]))
+        nc.scalar.dma_start(bias_all[:], bias.to_broadcast([P, N]))
 
         minus_mean_of = held.tile([P, P], BF16, name="minus_mean_of")
-        nc.gpsimd.memset(minus_mean_of[:], -1.0 / (ROWS * S))
+        nc.vector.memset(minus_mean_of[:], -1.0 / (ROWS * S))
         variance_of = held.tile([P, P], F32, name="variance_of")
-        nc.gpsimd.memset(variance_of[:], 1.0 / (ROWS * S - 1))
+        nc.vector.memset(variance_of[:], 1.0 / (ROWS * S - 1))
         eps = held.tile([P, 1], F32, name="eps")
-        nc.gpsimd.memset(eps[:], EPS)
+        nc.vector.memset(eps[:], EPS)
 
         warm = held.tile([P, 1], F32, name="warm")
         nc.scalar.activation(warm[:], eps[:], FUNC.Abs_reciprocal_sqrt)
 
         weight_f = held.tile([P, N], F32, name="weight_f")
-        nc.gpsimd.tensor_copy(weight_f[:], weight_bf[:])
+        nc.scalar.copy(weight_f[:], weight_bf[:])
 
         column_sums = psum.tile([P, S], F32, name="column_sums")
         for b in range(BLOCKS):

@@ -17,26 +17,29 @@ def tile_adaptivegroupnorm_kernel(tc, x, weight, bias, offs, out):
         tc.psum_pool(name="psum", bufs=1) as psum,
     ):
         x_bf = held.tile([P, BLOCKS * S], BF16, name="x_bf")
-        nc.sync.dma_start(x_bf[:].rearrange("p (b s) -> p b s", b=BLOCKS), x.rearrange("(b p) s -> p b s", p=P))
+        nc.sync.dma_start(x_bf[:, 0:S], x[0:P, :])
+        nc.scalar.dma_start(x_bf[:, S : 2 * S], x[P : 2 * P, :])
         offsets = held.tile([P, N // 16], U16, name="offsets")
         nc.sync.dma_start(offsets[:], offs)
         weight_bf = held.tile([P, N], BF16, name="weight_bf")
         nc.scalar.dma_start(weight_bf[:], weight.to_broadcast([P, N]))
-        bias_all = held.tile([P, N], F32, name="bias_all")
-        nc.scalar.dma_start(bias_all[:], bias.to_broadcast([P, N]))
+        bias_row = held.tile([1, N], F32, name="bias_row")
+        nc.sync.dma_start(bias_row[:], bias)
 
         minus_mean_of = held.tile([P, P], BF16, name="minus_mean_of")
-        nc.vector.memset(minus_mean_of[:], -1.0 / (ROWS * S))
+        nc.gpsimd.memset(minus_mean_of[:], -1.0 / (ROWS * S))
         variance_of = held.tile([P, P], F32, name="variance_of")
-        nc.vector.memset(variance_of[:], 1.0 / (ROWS * S - 1))
+        nc.gpsimd.memset(variance_of[:], 1.0 / (ROWS * S - 1))
         eps = held.tile([P, 1], F32, name="eps")
-        nc.vector.memset(eps[:], EPS)
+        nc.gpsimd.memset(eps[:], EPS)
+        ones_row = held.tile([1, P], F32, name="ones_row")
+        nc.gpsimd.memset(ones_row[:], 1.0)
 
         warm = held.tile([P, 1], F32, name="warm")
         nc.scalar.activation(warm[:], eps[:], FUNC.Abs_reciprocal_sqrt)
 
         weight_f = held.tile([P, N], F32, name="weight_f")
-        nc.scalar.copy(weight_f[:], weight_bf[:])
+        nc.gpsimd.tensor_copy(weight_f[:], weight_bf[:])
 
         column_sums = psum.tile([P, S], F32, name="column_sums")
         for b in range(BLOCKS):
@@ -46,6 +49,9 @@ def tile_adaptivegroupnorm_kernel(tc, x, weight, bias, offs, out):
         unused_copy = held.tile([P, S], F32, name="unused_copy")
         minus_mean = held.tile([P, 1], F32, name="minus_mean")
         nc.scalar.activation(unused_copy[:], column_sums[:], FUNC.Copy, accum_out=minus_mean[:])
+
+        bias_all = psum.tile([P, N], F32, name="bias_all")
+        nc.tensor.matmul(bias_all[:], ones_row[:], bias_row[:], start=True, stop=True)
 
         unused_squares = held.tile([P, BLOCKS * S], BF16, name="unused_squares")
         row_squares = held.tile([P, 1], F32, name="row_squares")

@@ -3,6 +3,7 @@ import concourse.mybir as mybir
 P = 128
 ROWS, S, N = 256, 256, 256
 BLOCKS = ROWS // P
+FOLD = 128
 EPS = 1e-5
 
 BF16, F32, U16 = mybir.dt.bfloat16, mybir.dt.float32, mybir.dt.uint16
@@ -23,8 +24,8 @@ def tile_adaptivegroupnorm_kernel(tc, x, weight, bias, offs, out):
         nc.sync.dma_start(offsets[:], offs)
         weight_bf = held.tile([P, N], BF16, name="weight_bf")
         nc.scalar.dma_start(weight_bf[:], weight.to_broadcast([P, N]))
-        bias_row = held.tile([1, N], F32, name="bias_row")
-        nc.sync.dma_start(bias_row[:], bias)
+        bias_all = held.tile([P, N], F32, name="bias_all")
+        nc.gpsimd.dma_start(bias_all[:], bias.to_broadcast([P, N]))
 
         minus_mean_of = held.tile([P, P], BF16, name="minus_mean_of")
         nc.gpsimd.memset(minus_mean_of[:], -1.0 / (ROWS * S))
@@ -32,8 +33,6 @@ def tile_adaptivegroupnorm_kernel(tc, x, weight, bias, offs, out):
         nc.gpsimd.memset(variance_of[:], 1.0 / (ROWS * S - 1))
         eps = held.tile([P, 1], F32, name="eps")
         nc.gpsimd.memset(eps[:], EPS)
-        ones_row = held.tile([1, P], F32, name="ones_row")
-        nc.gpsimd.memset(ones_row[:], 1.0)
 
         warm = held.tile([P, 1], F32, name="warm")
         nc.scalar.activation(warm[:], eps[:], FUNC.Abs_reciprocal_sqrt)
@@ -41,17 +40,15 @@ def tile_adaptivegroupnorm_kernel(tc, x, weight, bias, offs, out):
         weight_f = held.tile([P, N], F32, name="weight_f")
         nc.gpsimd.tensor_copy(weight_f[:], weight_bf[:])
 
-        column_sums = psum.tile([P, S], F32, name="column_sums")
-        for b in range(BLOCKS):
+        chunks = BLOCKS * S // FOLD
+        column_sums = psum.tile([P, FOLD], F32, name="column_sums")
+        for c in range(chunks):
             nc.tensor.matmul(
-                column_sums[:], minus_mean_of[:], x_bf[:, b * S : (b + 1) * S], start=(b == 0), stop=(b == BLOCKS - 1)
+                column_sums[:], minus_mean_of[:], x_bf[:, c * FOLD : (c + 1) * FOLD], start=(c == 0), stop=(c == chunks - 1)
             )
-        unused_copy = held.tile([P, S], F32, name="unused_copy")
+        unused_copy = held.tile([P, FOLD], F32, name="unused_copy")
         minus_mean = held.tile([P, 1], F32, name="minus_mean")
         nc.scalar.activation(unused_copy[:], column_sums[:], FUNC.Copy, accum_out=minus_mean[:])
-
-        bias_all = psum.tile([P, N], F32, name="bias_all")
-        nc.tensor.matmul(bias_all[:], ones_row[:], bias_row[:], start=True, stop=True)
 
         unused_squares = held.tile([P, BLOCKS * S], BF16, name="unused_squares")
         row_squares = held.tile([P, 1], F32, name="row_squares")
@@ -68,6 +65,7 @@ def tile_adaptivegroupnorm_kernel(tc, x, weight, bias, offs, out):
         result = [held.tile([P, N], F32, name=f"result{b}") for b in blocks]
         for b in blocks:
             nc.vector.tensor_copy(x_f[b][:], x_bf[:, b * S : (b + 1) * S])
+        for b in blocks:
             nc.vector.tensor_tensor(product[b][:], x_f[b][:].indirect(offsets[:]), weight_f[:], MULT)
         for b in blocks:
             nc.vector.scalar_tensor_tensor(centred[b][:], weight_f[:], minus_mean[:], product[b][:], MULT, ADD)

@@ -3,7 +3,7 @@ import concourse.mybir as mybir
 P = 128
 ROWS, S, N = 256, 256, 256
 BLOCKS = ROWS // P
-FOLD = 128
+WARM_MATMULS = 16
 EPS = 1e-5
 
 BF16, F32, U16 = mybir.dt.bfloat16, mybir.dt.float32, mybir.dt.uint16
@@ -40,13 +40,16 @@ def tile_adaptivegroupnorm_kernel(tc, x, weight, bias, offs, out):
         weight_f = held.tile([P, N], F32, name="weight_f")
         nc.gpsimd.tensor_copy(weight_f[:], weight_bf[:])
 
-        chunks = BLOCKS * S // FOLD
-        column_sums = psum.tile([P, FOLD], F32, name="column_sums")
-        for c in range(chunks):
+        idle_work = psum.tile([P, P], F32, name="idle_work")
+        for i in range(WARM_MATMULS):
+            nc.tensor.matmul(idle_work[:], minus_mean_of[:], minus_mean_of[:], start=True, stop=True)
+
+        column_sums = psum.tile([P, S], F32, name="column_sums")
+        for b in range(BLOCKS):
             nc.tensor.matmul(
-                column_sums[:], minus_mean_of[:], x_bf[:, c * FOLD : (c + 1) * FOLD], start=(c == 0), stop=(c == chunks - 1)
+                column_sums[:], minus_mean_of[:], x_bf[:, b * S : (b + 1) * S], start=(b == 0), stop=(b == BLOCKS - 1)
             )
-        unused_copy = held.tile([P, FOLD], F32, name="unused_copy")
+        unused_copy = held.tile([P, S], F32, name="unused_copy")
         minus_mean = held.tile([P, 1], F32, name="minus_mean")
         nc.scalar.activation(unused_copy[:], column_sums[:], FUNC.Copy, accum_out=minus_mean[:])
 

@@ -3,7 +3,7 @@ import concourse.mybir as mybir
 P = 128
 ROWS, S, N = 256, 256, 256
 BLOCKS = ROWS // P
-WARM_MATMULS = 16
+M = BLOCKS * S
 EPS = 1e-5
 
 BF16, F32, U16 = mybir.dt.bfloat16, mybir.dt.float32, mybir.dt.uint16
@@ -13,11 +13,12 @@ FUNC = mybir.ActivationFunctionType
 
 def tile_adaptivegroupnorm_kernel(tc, x, weight, bias, offs, out):
     nc = tc.nc
+    blocks = range(BLOCKS)
     with (
         tc.tile_pool(name="held", bufs=1) as held,
         tc.psum_pool(name="psum", bufs=1) as psum,
     ):
-        x_bf = held.tile([P, BLOCKS * S], BF16, name="x_bf")
+        x_bf = held.tile([P, M], BF16, name="x_bf")
         nc.sync.dma_start(x_bf[:, 0:S], x[0:P, :])
         nc.scalar.dma_start(x_bf[:, S : 2 * S], x[P : 2 * P, :])
         offsets = held.tile([P, N // 16], U16, name="offsets")
@@ -30,7 +31,7 @@ def tile_adaptivegroupnorm_kernel(tc, x, weight, bias, offs, out):
         minus_mean_of = held.tile([P, P], BF16, name="minus_mean_of")
         nc.gpsimd.memset(minus_mean_of[:], -1.0 / (ROWS * S))
         variance_of = held.tile([P, P], F32, name="variance_of")
-        nc.gpsimd.memset(variance_of[:], 1.0 / (ROWS * S - 1))
+        nc.gpsimd.memset(variance_of[:], M / (ROWS * S - 1))
         eps = held.tile([P, 1], F32, name="eps")
         nc.gpsimd.memset(eps[:], EPS)
 
@@ -40,34 +41,34 @@ def tile_adaptivegroupnorm_kernel(tc, x, weight, bias, offs, out):
         weight_f = held.tile([P, N], F32, name="weight_f")
         nc.gpsimd.tensor_copy(weight_f[:], weight_bf[:])
 
-        idle_work = psum.tile([P, P], F32, name="idle_work")
-        for i in range(WARM_MATMULS):
-            nc.tensor.matmul(idle_work[:], minus_mean_of[:], minus_mean_of[:], start=True, stop=True)
+        partition_stats = held.tile([P, 6], F32, name="partition_stats")
+        nc.vector.bn_stats(partition_stats[:], x_bf[:])
+        mean_var_p = held.tile([P, 2], F32, name="mean_var_p")
+        nc.vector.bn_aggr(mean_var_p[:], partition_stats[:])
 
         column_sums = psum.tile([P, S], F32, name="column_sums")
-        for b in range(BLOCKS):
+        for b in blocks:
             nc.tensor.matmul(
                 column_sums[:], minus_mean_of[:], x_bf[:, b * S : (b + 1) * S], start=(b == 0), stop=(b == BLOCKS - 1)
             )
+        x_f = [held.tile([P, S], F32, name=f"x_f{b}") for b in blocks]
+        for b in blocks:
+            nc.scalar.copy(x_f[b][:], x_bf[:, b * S : (b + 1) * S])
         unused_copy = held.tile([P, S], F32, name="unused_copy")
         minus_mean = held.tile([P, 1], F32, name="minus_mean")
         nc.scalar.activation(unused_copy[:], column_sums[:], FUNC.Copy, accum_out=minus_mean[:])
 
-        unused_squares = held.tile([P, BLOCKS * S], BF16, name="unused_squares")
-        row_squares = held.tile([P, 1], F32, name="row_squares")
-        nc.scalar.activation(unused_squares[:], x_bf[:], FUNC.Square, bias=minus_mean[:], accum_out=row_squares[:])
         variance = psum.tile([P, 1], F32, name="variance")
-        nc.tensor.matmul(variance[:], variance_of[:], row_squares[:], start=True, stop=True)
+        nc.tensor.matmul(variance[:], variance_of[:], mean_var_p[:, 1:2], start=True, stop=False)
+        deviation_sq = held.tile([P, 1], F32, name="deviation_sq")
+        nc.scalar.activation(deviation_sq[:], mean_var_p[:, 0:1], FUNC.Square, bias=minus_mean[:])
+        nc.tensor.matmul(variance[:], variance_of[:], deviation_sq[:], start=False, stop=True)
         rstd = held.tile([P, 1], F32, name="rstd")
         nc.scalar.activation(rstd[:], variance[:], FUNC.Abs_reciprocal_sqrt, bias=eps[:])
 
-        blocks = range(BLOCKS)
-        x_f = [held.tile([P, S], F32, name=f"x_f{b}") for b in blocks]
         product = [held.tile([P, N], F32, name=f"product{b}") for b in blocks]
         centred = [held.tile([P, N], F32, name=f"centred{b}") for b in blocks]
         result = [held.tile([P, N], F32, name=f"result{b}") for b in blocks]
-        for b in blocks:
-            nc.vector.tensor_copy(x_f[b][:], x_bf[:, b * S : (b + 1) * S])
         for b in blocks:
             nc.vector.tensor_tensor(product[b][:], x_f[b][:].indirect(offsets[:]), weight_f[:], MULT)
         for b in blocks:

@@ -3,7 +3,7 @@ import concourse.mybir as mybir
 P = 128
 ROWS, S, N = 256, 256, 256
 BLOCKS = ROWS // P
-M = BLOCKS * S
+FOLD = 128
 EPS = 1e-5
 
 BF16, F32, U16 = mybir.dt.bfloat16, mybir.dt.float32, mybir.dt.uint16
@@ -13,56 +13,52 @@ FUNC = mybir.ActivationFunctionType
 
 def tile_adaptivegroupnorm_kernel(tc, x, weight, bias, offs, out):
     nc = tc.nc
-    blocks = range(BLOCKS)
     with (
         tc.tile_pool(name="held", bufs=1) as held,
         tc.psum_pool(name="psum", bufs=1) as psum,
     ):
-        x_bf = held.tile([P, M], BF16, name="x_bf")
-        nc.sync.dma_start(x_bf[:, 0:S], x[0:P, :])
-        nc.scalar.dma_start(x_bf[:, S : 2 * S], x[P : 2 * P, :])
-        offsets = held.tile([P, N // 16], U16, name="offsets")
-        nc.sync.dma_start(offsets[:], offs)
+        x_bf = held.tile([P, BLOCKS * S], BF16, name="x_bf")
         weight_bf = held.tile([P, N], BF16, name="weight_bf")
+        offsets = held.tile([P, N // 16], U16, name="offsets")
+        nc.sync.dma_start(x_bf[:, 0:S], x[0:P, :])
         nc.scalar.dma_start(weight_bf[:], weight.to_broadcast([P, N]))
+        nc.sync.dma_start(offsets[:], offs)
+        nc.scalar.dma_start(x_bf[:, S : 2 * S], x[P : 2 * P, :])
         bias_all = held.tile([P, N], F32, name="bias_all")
         nc.gpsimd.dma_start(bias_all[:], bias.to_broadcast([P, N]))
 
         minus_mean_of = held.tile([P, P], BF16, name="minus_mean_of")
         nc.gpsimd.memset(minus_mean_of[:], -1.0 / (ROWS * S))
         variance_of = held.tile([P, P], F32, name="variance_of")
-        nc.gpsimd.memset(variance_of[:], M / (ROWS * S - 1))
+        nc.gpsimd.memset(variance_of[:], 1.0 / (ROWS * S - 1))
         eps = held.tile([P, 1], F32, name="eps")
         nc.gpsimd.memset(eps[:], EPS)
 
         warm = held.tile([P, 1], F32, name="warm")
         nc.scalar.activation(warm[:], eps[:], FUNC.Abs_reciprocal_sqrt)
 
-        weight_f = held.tile([P, N], F32, name="weight_f")
-        nc.gpsimd.tensor_copy(weight_f[:], weight_bf[:])
-
-        partition_stats = held.tile([P, 6], F32, name="partition_stats")
-        nc.vector.bn_stats(partition_stats[:], x_bf[:])
-        mean_var_p = held.tile([P, 2], F32, name="mean_var_p")
-        nc.vector.bn_aggr(mean_var_p[:], partition_stats[:])
-
-        column_sums = psum.tile([P, S], F32, name="column_sums")
-        for b in blocks:
-            nc.tensor.matmul(
-                column_sums[:], minus_mean_of[:], x_bf[:, b * S : (b + 1) * S], start=(b == 0), stop=(b == BLOCKS - 1)
-            )
+        blocks = range(BLOCKS)
         x_f = [held.tile([P, S], F32, name=f"x_f{b}") for b in blocks]
-        for b in blocks:
-            nc.scalar.copy(x_f[b][:], x_bf[:, b * S : (b + 1) * S])
-        unused_copy = held.tile([P, S], F32, name="unused_copy")
+        weight_f = held.tile([P, N], F32, name="weight_f")
+        nc.vector.tensor_copy(x_f[0][:], x_bf[:, 0:S])
+        nc.vector.tensor_copy(weight_f[:], weight_bf[:])
+        nc.scalar.copy(x_f[1][:], x_bf[:, S : 2 * S])
+
+        chunks = BLOCKS * S // FOLD
+        column_sums = psum.tile([P, FOLD], F32, name="column_sums")
+        for c in range(chunks):
+            nc.tensor.matmul(
+                column_sums[:], minus_mean_of[:], x_bf[:, c * FOLD : (c + 1) * FOLD], start=(c == 0), stop=(c == chunks - 1)
+            )
+        unused_copy = held.tile([P, FOLD], F32, name="unused_copy")
         minus_mean = held.tile([P, 1], F32, name="minus_mean")
         nc.scalar.activation(unused_copy[:], column_sums[:], FUNC.Copy, accum_out=minus_mean[:])
 
+        unused_squares = held.tile([P, BLOCKS * S], BF16, name="unused_squares")
+        row_squares = held.tile([P, 1], F32, name="row_squares")
+        nc.scalar.activation(unused_squares[:], x_bf[:], FUNC.Square, bias=minus_mean[:], accum_out=row_squares[:])
         variance = psum.tile([P, 1], F32, name="variance")
-        nc.tensor.matmul(variance[:], variance_of[:], mean_var_p[:, 1:2], start=True, stop=False)
-        deviation_sq = held.tile([P, 1], F32, name="deviation_sq")
-        nc.scalar.activation(deviation_sq[:], mean_var_p[:, 0:1], FUNC.Square, bias=minus_mean[:])
-        nc.tensor.matmul(variance[:], variance_of[:], deviation_sq[:], start=False, stop=True)
+        nc.tensor.matmul(variance[:], variance_of[:], row_squares[:], start=True, stop=True)
         rstd = held.tile([P, 1], F32, name="rstd")
         nc.scalar.activation(rstd[:], variance[:], FUNC.Abs_reciprocal_sqrt, bias=eps[:])
 

@@ -4,6 +4,7 @@ P = 128
 ROWS, S, N = 256, 256, 256
 BLOCKS = ROWS // P
 FOLD = 128
+WARM_MATMULS = 16
 EPS = 1e-5
 
 BF16, F32, U16 = mybir.dt.bfloat16, mybir.dt.float32, mybir.dt.uint16
@@ -18,31 +19,28 @@ def tile_adaptivegroupnorm_kernel(tc, x, weight, bias, offs, out):
         tc.psum_pool(name="psum", bufs=1) as psum,
     ):
         x_bf = held.tile([P, BLOCKS * S], BF16, name="x_bf")
-        weight_bf = held.tile([P, N], BF16, name="weight_bf")
-        offsets = held.tile([P, N // 16], U16, name="offsets")
         nc.sync.dma_start(x_bf[:, 0:S], x[0:P, :])
-        nc.scalar.dma_start(weight_bf[:], weight.to_broadcast([P, N]))
-        nc.sync.dma_start(offsets[:], offs)
         nc.scalar.dma_start(x_bf[:, S : 2 * S], x[P : 2 * P, :])
+        offsets = held.tile([P, N // 16], U16, name="offsets")
+        nc.sync.dma_start(offsets[:], offs)
+        weight_bf = held.tile([P, N], BF16, name="weight_bf")
+        nc.scalar.dma_start(weight_bf[:], weight.to_broadcast([P, N]))
         bias_all = held.tile([P, N], F32, name="bias_all")
         nc.gpsimd.dma_start(bias_all[:], bias.to_broadcast([P, N]))
 
         minus_mean_of = held.tile([P, P], BF16, name="minus_mean_of")
-        nc.gpsimd.memset(minus_mean_of[:], -1.0 / (ROWS * S))
+        nc.vector.memset(minus_mean_of[:], -1.0 / (ROWS * S))
         variance_of = held.tile([P, P], F32, name="variance_of")
-        nc.gpsimd.memset(variance_of[:], 1.0 / (ROWS * S - 1))
+        nc.vector.memset(variance_of[:], 1.0 / (ROWS * S - 1))
         eps = held.tile([P, 1], F32, name="eps")
-        nc.gpsimd.memset(eps[:], EPS)
+        nc.vector.memset(eps[:], EPS)
 
         warm = held.tile([P, 1], F32, name="warm")
         nc.scalar.activation(warm[:], eps[:], FUNC.Abs_reciprocal_sqrt)
 
-        blocks = range(BLOCKS)
-        x_f = [held.tile([P, S], F32, name=f"x_f{b}") for b in blocks]
-        weight_f = held.tile([P, N], F32, name="weight_f")
-        nc.vector.tensor_copy(x_f[0][:], x_bf[:, 0:S])
-        nc.vector.tensor_copy(weight_f[:], weight_bf[:])
-        nc.scalar.copy(x_f[1][:], x_bf[:, S : 2 * S])
+        idle_work = psum.tile([P, P], F32, name="idle_work")
+        for i in range(WARM_MATMULS):
+            nc.tensor.matmul(idle_work[:], minus_mean_of[:], minus_mean_of[:], start=True, stop=True)
 
         chunks = BLOCKS * S // FOLD
         column_sums = psum.tile([P, FOLD], F32, name="column_sums")
@@ -62,9 +60,15 @@ def tile_adaptivegroupnorm_kernel(tc, x, weight, bias, offs, out):
         rstd = held.tile([P, 1], F32, name="rstd")
         nc.scalar.activation(rstd[:], variance[:], FUNC.Abs_reciprocal_sqrt, bias=eps[:])
 
+        blocks = range(BLOCKS)
+        x_f = [held.tile([P, S], F32, name=f"x_f{b}") for b in blocks]
         product = [held.tile([P, N], F32, name=f"product{b}") for b in blocks]
         centred = [held.tile([P, N], F32, name=f"centred{b}") for b in blocks]
         result = [held.tile([P, N], F32, name=f"result{b}") for b in blocks]
+        for b in blocks:
+            nc.vector.tensor_copy(x_f[b][:], x_bf[:, b * S : (b + 1) * S])
+        weight_f = held.tile([P, N], F32, name="weight_f")
+        nc.vector.tensor_copy(weight_f[:], weight_bf[:])
         for b in blocks:
             nc.vector.tensor_tensor(product[b][:], x_f[b][:].indirect(offsets[:]), weight_f[:], MULT)
         for b in blocks:

@@ -1,11 +1,17 @@
+import math
+
 import concourse.mybir as mybir
 
 P = 128
 ROWS, S, N = 256, 256, 256
 BLOCKS = ROWS // P
+COUNT = ROWS * S
+PILOT = 64
 FOLD = 128
+BANK = 512
 WARM_MATMULS = 16
 EPS = 1e-5
+ROOT = math.sqrt(COUNT / (COUNT - 1))
 
 BF16, F32, U16 = mybir.dt.bfloat16, mybir.dt.float32, mybir.dt.uint16
 MULT, ADD = mybir.AluOpType.mult, mybir.AluOpType.add
@@ -18,6 +24,8 @@ def tile_adaptivegroupnorm_kernel(tc, x, weight, bias, offs, out):
         tc.tile_pool(name="held", bufs=1) as held,
         tc.psum_pool(name="psum", bufs=1) as psum,
     ):
+        pilot = held.tile([P, PILOT], BF16, name="pilot")
+        nc.sync.dma_start(pilot[:], x[0:1, 0:PILOT].to_broadcast([P, PILOT]))
         x_bf = held.tile([P, BLOCKS * S], BF16, name="x_bf")
         nc.sync.dma_start(x_bf[:, 0:S], x[0:P, :])
         nc.scalar.dma_start(x_bf[:, S : 2 * S], x[P : 2 * P, :])
@@ -29,18 +37,31 @@ def tile_adaptivegroupnorm_kernel(tc, x, weight, bias, offs, out):
         nc.gpsimd.dma_start(bias_all[:], bias.to_broadcast([P, N]))
 
         minus_mean_of = held.tile([P, P], BF16, name="minus_mean_of")
-        nc.vector.memset(minus_mean_of[:], -1.0 / (ROWS * S))
-        variance_of = held.tile([P, P], F32, name="variance_of")
-        nc.vector.memset(variance_of[:], 1.0 / (ROWS * S - 1))
-        eps = held.tile([P, 1], F32, name="eps")
-        nc.vector.memset(eps[:], EPS)
+        nc.vector.memset(minus_mean_of[:], -1.0 / COUNT)
+        mean_of = held.tile([P, P], F32, name="mean_of")
+        nc.vector.memset(mean_of[:], 1.0 / COUNT)
+        eps_share = held.tile([P, 1], F32, name="eps_share")
+        nc.vector.memset(eps_share[:], EPS * COUNT / P)
 
         warm = held.tile([P, 1], F32, name="warm")
-        nc.scalar.activation(warm[:], eps[:], FUNC.Abs_reciprocal_sqrt)
+        nc.scalar.activation(warm[:], eps_share[:], FUNC.Abs_reciprocal_sqrt)
+
+        spread = psum.tile([P, BANK], F32, name="spread")
+        nc.tensor.matmul(spread[:, 0:1], mean_of[:], eps_share[:], start=True, stop=False)
 
         idle_work = psum.tile([P, P], F32, name="idle_work")
         for i in range(WARM_MATMULS):
             nc.tensor.matmul(idle_work[:], minus_mean_of[:], minus_mean_of[:], start=True, stop=True)
+
+        unused_pilot = held.tile([P, PILOT], F32, name="unused_pilot")
+        minus_pilot = held.tile([P, 1], F32, name="minus_pilot")
+        nc.scalar.activation(unused_pilot[:], pilot[:], FUNC.Copy, scale=-ROOT / PILOT, accum_out=minus_pilot[:])
+
+        unused_squares = held.tile([P, BLOCKS * S], BF16, name="unused_squares")
+        row_squares = held.tile([P, 1], F32, name="row_squares")
+        nc.scalar.activation(
+            unused_squares[:], x_bf[:], FUNC.Square, bias=minus_pilot[:], scale=ROOT, accum_out=row_squares[:]
+        )
 
         chunks = BLOCKS * S // FOLD
         column_sums = psum.tile([P, FOLD], F32, name="column_sums")
@@ -52,13 +73,12 @@ def tile_adaptivegroupnorm_kernel(tc, x, weight, bias, offs, out):
         minus_mean = held.tile([P, 1], F32, name="minus_mean")
         nc.scalar.activation(unused_copy[:], column_sums[:], FUNC.Copy, accum_out=minus_mean[:])
 
-        unused_squares = held.tile([P, BLOCKS * S], BF16, name="unused_squares")
-        row_squares = held.tile([P, 1], F32, name="row_squares")
-        nc.scalar.activation(unused_squares[:], x_bf[:], FUNC.Square, bias=minus_mean[:], accum_out=row_squares[:])
-        variance = psum.tile([P, 1], F32, name="variance")
-        nc.tensor.matmul(variance[:], variance_of[:], row_squares[:], start=True, stop=True)
+        nc.tensor.matmul(spread[:, 0:1], mean_of[:], row_squares[:], start=False, stop=True)
+
+        shift = held.tile([P, 1], F32, name="shift")
+        nc.scalar.activation(shift[:], minus_mean[:], FUNC.Square, bias=minus_pilot[:], scale=-ROOT)
         rstd = held.tile([P, 1], F32, name="rstd")
-        nc.scalar.activation(rstd[:], variance[:], FUNC.Abs_reciprocal_sqrt, bias=eps[:])
+        nc.scalar.activation(rstd[:], spread[:, 0:1], FUNC.Abs_reciprocal_sqrt, bias=shift[:], scale=-1.0)
 
         blocks = range(BLOCKS)
         x_f = [held.tile([P, S], F32, name=f"x_f{b}") for b in blocks]

@@ -27,8 +27,7 @@ def tile_adaptivegroupnorm_kernel(tc, x, weight, bias, offs, out):
         pilot = held.tile([P, PILOT], BF16, name="pilot")
         nc.sync.dma_start(pilot[:], x[0:1, 0:PILOT].to_broadcast([P, PILOT]))
         x_bf = held.tile([P, BLOCKS * S], BF16, name="x_bf")
-        nc.sync.dma_start(x_bf[:, 0:S], x[0:P, :])
-        nc.scalar.dma_start(x_bf[:, S : 2 * S], x[P : 2 * P, :])
+        nc.sync.dma_start(x_bf[:], x.rearrange("(q b) s -> q (b s)", b=BLOCKS))
         offsets = held.tile([P, N // 16], U16, name="offsets")
         nc.sync.dma_start(offsets[:], offs)
         weight_bf = held.tile([P, N], BF16, name="weight_bf")
@@ -93,7 +92,8 @@ def tile_adaptivegroupnorm_kernel(tc, x, weight, bias, offs, out):
             nc.vector.tensor_tensor(product[b][:], x_f[b][:].indirect(offsets[:]), weight_f[:], MULT)
         for b in blocks:
             nc.vector.scalar_tensor_tensor(centred[b][:], weight_f[:], minus_mean[:], product[b][:], MULT, ADD)
+        out_blocks = out.rearrange("(q b) n -> b q n", b=BLOCKS)
         store_queues = [nc.sync, nc.scalar]
         for b in blocks:
             nc.vector.scalar_tensor_tensor(result[b][:], centred[b][:], rstd[:], bias_all[:], MULT, ADD)
-            store_queues[b].dma_start(out[b * P : (b + 1) * P, :], result[b][:])
+            store_queues[b].dma_start(out_blocks[b, :, :], result[b][:])

@@ -9,7 +9,6 @@ COUNT = ROWS * S
 PILOT = 64
 FOLD = 128
 BANK = 512
-WARM_MATMULS = 16
 EPS = 1e-5
 ROOT = math.sqrt(COUNT / (COUNT - 1))
 
@@ -47,10 +46,6 @@ def tile_adaptivegroupnorm_kernel(tc, x, weight, bias, offs, out):
 
         spread = psum.tile([P, BANK], F32, name="spread")
         nc.tensor.matmul(spread[:, 0:1], mean_of[:], eps_share[:], start=True, stop=False)
-
-        idle_work = psum.tile([P, P], F32, name="idle_work")
-        for i in range(WARM_MATMULS):
-            nc.tensor.matmul(idle_work[:], minus_mean_of[:], minus_mean_of[:], start=True, stop=True)
 
         unused_pilot = held.tile([P, PILOT], F32, name="unused_pilot")
         minus_pilot = held.tile([P, 1], F32, name="minus_pilot")

@@ -23,14 +23,14 @@ def tile_adaptivegroupnorm_kernel(tc, x, weight, bias, offs, out):
         tc.tile_pool(name="held", bufs=1) as held,
         tc.psum_pool(name="psum", bufs=1) as psum,
     ):
+        weight_bf = held.tile([P, N], BF16, name="weight_bf")
+        nc.sync.dma_start(weight_bf[:], weight.to_broadcast([P, N]))
         pilot = held.tile([P, PILOT], BF16, name="pilot")
-        nc.sync.dma_start(pilot[:], x[0:1, 0:PILOT].to_broadcast([P, PILOT]))
+        nc.scalar.dma_start(pilot[:], x[0:1, 0:PILOT].to_broadcast([P, PILOT]))
         x_bf = held.tile([P, BLOCKS * S], BF16, name="x_bf")
         nc.sync.dma_start(x_bf[:], x.rearrange("(q b) s -> q (b s)", b=BLOCKS))
         offsets = held.tile([P, N // 16], U16, name="offsets")
         nc.sync.dma_start(offsets[:], offs)
-        weight_bf = held.tile([P, N], BF16, name="weight_bf")
-        nc.scalar.dma_start(weight_bf[:], weight.to_broadcast([P, N]))
         bias_all = held.tile([P, N], F32, name="bias_all")
         nc.gpsimd.dma_start(bias_all[:], bias.to_broadcast([P, N]))
 

import math

import concourse.mybir as mybir

P = 128
ROWS, S, N = 256, 256, 256
BLOCKS = ROWS // P
COUNT = ROWS * S
PILOT = 64
FOLD = 128
BANK = 512
EPS = 1e-5
ROOT = math.sqrt(COUNT / (COUNT - 1))

BF16, F32, U16 = mybir.dt.bfloat16, mybir.dt.float32, mybir.dt.uint16
MULT, ADD = mybir.AluOpType.mult, mybir.AluOpType.add
FUNC = mybir.ActivationFunctionType


def tile_adaptivegroupnorm_kernel(tc, x, weight, bias, offs, out):
    nc = tc.nc
    with (
        tc.tile_pool(name="held", bufs=1) as held,
        tc.psum_pool(name="psum", bufs=1) as psum,
    ):
        weight_bf = held.tile([P, N], BF16, name="weight_bf")
        nc.sync.dma_start(weight_bf[:], weight.to_broadcast([P, N]))
        pilot = held.tile([P, PILOT], BF16, name="pilot")
        nc.scalar.dma_start(pilot[:], x[0:1, 0:PILOT].to_broadcast([P, PILOT]))
        x_bf = held.tile([P, BLOCKS * S], BF16, name="x_bf")
        nc.sync.dma_start(x_bf[:], x.rearrange("(q b) s -> q (b s)", b=BLOCKS))
        offsets = held.tile([P, N // 16], U16, name="offsets")
        nc.sync.dma_start(offsets[:], offs)
        bias_all = held.tile([P, N], F32, name="bias_all")
        nc.gpsimd.dma_start(bias_all[:], bias.to_broadcast([P, N]))

        minus_mean_of = held.tile([P, P], BF16, name="minus_mean_of")
        nc.vector.memset(minus_mean_of[:], -1.0 / COUNT)
        mean_of = held.tile([P, P], F32, name="mean_of")
        nc.vector.memset(mean_of[:], 1.0 / COUNT)
        eps_share = held.tile([P, 1], F32, name="eps_share")
        nc.vector.memset(eps_share[:], EPS * COUNT / P)

        warm = held.tile([P, 1], F32, name="warm")
        nc.scalar.activation(warm[:], eps_share[:], FUNC.Abs_reciprocal_sqrt)

        spread = psum.tile([P, BANK], F32, name="spread")
        nc.tensor.matmul(spread[:, 0:1], mean_of[:], eps_share[:], start=True, stop=False)

        unused_pilot = held.tile([P, PILOT], F32, name="unused_pilot")
        minus_pilot = held.tile([P, 1], F32, name="minus_pilot")
        nc.scalar.activation(unused_pilot[:], pilot[:], FUNC.Copy, scale=-ROOT / PILOT, accum_out=minus_pilot[:])

        unused_squares = held.tile([P, BLOCKS * S], BF16, name="unused_squares")
        row_squares = held.tile([P, 1], F32, name="row_squares")
        nc.scalar.activation(
            unused_squares[:], x_bf[:], FUNC.Square, bias=minus_pilot[:], scale=ROOT, accum_out=row_squares[:]
        )

        chunks = BLOCKS * S // FOLD
        column_sums = psum.tile([P, FOLD], F32, name="column_sums")
        for c in range(chunks):
            nc.tensor.matmul(
                column_sums[:], minus_mean_of[:], x_bf[:, c * FOLD : (c + 1) * FOLD], start=(c == 0), stop=(c == chunks - 1)
            )
        unused_copy = held.tile([P, FOLD], F32, name="unused_copy")
        minus_mean = held.tile([P, 1], F32, name="minus_mean")
        nc.scalar.activation(unused_copy[:], column_sums[:], FUNC.Copy, accum_out=minus_mean[:])

        nc.tensor.matmul(spread[:, 0:1], mean_of[:], row_squares[:], start=False, stop=True)

        shift = held.tile([P, 1], F32, name="shift")
        nc.scalar.activation(shift[:], minus_mean[:], FUNC.Square, bias=minus_pilot[:], scale=-ROOT)
        rstd = held.tile([P, 1], F32, name="rstd")
        nc.scalar.activation(rstd[:], spread[:, 0:1], FUNC.Abs_reciprocal_sqrt, bias=shift[:], scale=-1.0)

        blocks = range(BLOCKS)
        x_f = [held.tile([P, S], F32, name=f"x_f{b}") for b in blocks]
        product = [held.tile([P, N], F32, name=f"product{b}") for b in blocks]
        centred = [held.tile([P, N], F32, name=f"centred{b}") for b in blocks]
        result = [held.tile([P, N], F32, name=f"result{b}") for b in blocks]
        for b in blocks:
            nc.vector.tensor_copy(x_f[b][:], x_bf[:, b * S : (b + 1) * S])
        weight_f = held.tile([P, N], F32, name="weight_f")
        nc.vector.tensor_copy(weight_f[:], weight_bf[:])
        for b in blocks:
            nc.vector.tensor_tensor(product[b][:], x_f[b][:].indirect(offsets[:]), weight_f[:], MULT)
        for b in blocks:
            nc.vector.scalar_tensor_tensor(centred[b][:], weight_f[:], minus_mean[:], product[b][:], MULT, ADD)
        out_blocks = out.rearrange("(q b) n -> b q n", b=BLOCKS)
        store_queues = [nc.sync, nc.scalar]
        for b in blocks:
            nc.vector.scalar_tensor_tensor(result[b][:], centred[b][:], rstd[:], bias_all[:], MULT, ADD)
            store_queues[b].dma_start(out_blocks[b, :, :], result[b][:])
